import numpy as np
import ml_dtypes


def mxq(x, axis, fmt="e4m3"):
    dtype, down = {"e4m3": (ml_dtypes.float8_e4m3fn, 7), "e5m2": (ml_dtypes.float8_e5m2, 14)}[fmt]
    v = np.moveaxis(np.asarray(x, np.float32).astype(ml_dtypes.bfloat16).astype(np.float64), axis, -1)
    blocks = v.reshape(v.shape[:-1] + (-1, 32))
    amax = np.abs(blocks).max(-1, keepdims=True)
    byte = np.maximum(np.where(amax > 0, np.frexp(amax)[1] - 1 + 127, 0) - down, 1)
    scale = np.exp2(byte - 127.0)
    codes = (blocks / scale).astype(np.float32).astype(dtype).astype(np.float64)
    return np.moveaxis((codes * scale).reshape(v.shape), -1, axis)


WIDE = False


def mx_kscale(k):
    if not WIDE:
        return np.ones(k)
    levels = np.array([18, -18])
    if k % 512:
        return np.exp2(np.random.permutation(np.resize(levels, k // 32))).repeat(32)
    a = np.empty((k // 512, 16))
    for p in range(k // 512):
        a[p, :8] = np.random.permutation(np.resize(levels, 8))
        for g in range(8):
            far = levels[np.abs(levels - a[p, g]) >= 10]
            a[p, g + 8] = far[np.random.randint(len(far))]
    return np.exp2(a.ravel()).repeat(32)


BF16 = ml_dtypes.bfloat16


def bf(x):
    return np.asarray(x, np.float32).astype(BF16)


def f64(x):
    return np.asarray(x).astype(np.float64)


B, CIN, CM, CO, H, WD = 8, 512, 512, 512, 8, 8
T = B * H * WD
RING = [(-1, -1), (-1, 0), (-1, 1), (0, 1), (1, 1), (1, 0), (1, -1), (0, -1)]
NUM_K = 9
KERNEL_ROT = 4
STEP = 2
M = NUM_K * CM


def offset(k, rot):
    return (0, 0) if k == NUM_K - 1 else RING[(k + STEP * rot) % len(RING)]


def setup_inputs():
    s = mx_kscale(T)[::H * WD]
    u = mx_kscale(CO)
    v = mx_kscale(M)
    x0 = bf(np.random.standard_normal((B, CIN, H, WD)))
    W0 = bf(np.random.standard_normal((CM, CIN, NUM_K)) / np.sqrt(CIN))
    W1_0 = bf(np.random.standard_normal((CO, M)) * 1.4 / np.sqrt(M))
    g = np.random.standard_normal((B, CO, KERNEL_ROT, H, WD)) * np.exp2(np.random.randint(-6, 1, (B, 1, 1, H, WD)))
    g = bf(g / s[:, None, None, None, None] * u[None, :, None, None, None])
    z = (f64(W0).transpose(0, 2, 1).reshape(CM * NUM_K, CIN) @ f64(x0).reshape(B, CIN, H * WD)).reshape(B, CM, NUM_K, H, WD)
    vok = v.reshape(NUM_K, CM).T
    return {"x": bf(f64(x0) * s[:, None, None, None]),
            "W": bf(f64(W0) / vok[:, None, :]),
            "W1": bf(f64(W1_0) * v[None, :] / u[:, None]),
            "z": np.asarray(z, np.float32),
            "grad_out": g}


def reference(x, W, W1, z, grad_out):
    gp = np.pad(f64(grad_out), ((0, 0), (0, 0), (0, 0), (1, 1), (1, 1)))
    parts = []
    for k in range(NUM_K):
        acc = 0.0
        for rot in range(KERNEL_ROT):
            dy, dx = offset(k, rot)
            acc = acc + gp[:, :, rot, 1 - dy:1 - dy + H, 1 - dx:1 - dx + WD]
        parts.append(acc.transpose(1, 0, 2, 3).reshape(CO, T))
    du = np.stack(parts, axis=0)
    duq = mxq(du, 1, "e5m2")
    W1q = mxq(f64(W1).reshape(CO, NUM_K, CM), 0, "e4m3")
    dh = (W1q.transpose(1, 2, 0) @ duq).reshape(M, T)
    zf = f64(z).transpose(2, 1, 0, 3, 4).reshape(M, T)
    dz = dh * (zf > 0.0)
    Wm = f64(W).transpose(2, 0, 1).reshape(M, CIN)
    gx = mxq(Wm, 0, "e4m3").T @ mxq(dz, 0, "e5m2")
    xt = f64(x).transpose(1, 0, 2, 3).reshape(CIN, T)
    gW = mxq(dz, 1, "e5m2") @ mxq(xt, 1, "e4m3").T
    return (gx.reshape(CIN, B, H, WD).transpose(1, 0, 2, 3),
            gW.reshape(NUM_K, CM, CIN).transpose(1, 2, 0))

@@ -1,0 +1,418 @@
+from contextlib import ExitStack
+
+import concourse.mybir as mybir
+from concourse.masks import make_identity
+
+F32 = mybir.dt.float32
+BF16 = mybir.dt.bfloat16
+U32 = mybir.dt.uint32
+U8 = mybir.dt.uint8
+E4M3 = mybir.dt.float8_e4m3fn_x4
+E5M2 = mybir.dt.float8_e5m2_x4
+ALU = mybir.AluOpType
+
+B, C, K9, ROT, S = 8, 512, 9, 4, 8
+T = B * S * S
+P = 128
+FLOPS = 3 * 2 * K9 * C * C * T
+RING = [(-1, -1), (-1, 0), (-1, 1), (0, 1), (1, 1), (1, 0), (1, -1), (0, -1)]
+SETS = [(0, 0, 3), (2, 1, 2), (4, 1, 3)]
+STEPS = 18
+S_W1 = ()
+KLAST = "vvsv"
+TENG = "v"
+
+
+def tile_psr4convf_v_kernel(tc, x, W, W1, z, grad_out, out_0, out_1):
+    nc = tc.nc
+    g_v = grad_out.rearrange("b (q j) r h w -> q b (j r h w)", j=4)
+    x_v = x.rearrange("b (p c) h w -> p b (c h w)", c=4)
+    w1_v = W1.rearrange("(p j) m -> p j m", j=4)
+    w_v = W.rearrange("(p j) c k -> p j (c k)", j=4)
+    z_v = z.rearrange("b (p j) k h w -> j p b (k h w)", j=4)
+    o1_v = out_1.rearrange("(p j) c k -> j p (c k)", j=4)
+    o0_v = out_0.rearrange("b (n p) h w -> n p b (h w)", p=P)
+
+    with ExitStack() as ctx:
+        const = ctx.enter_context(tc.tile_pool(name="const", bufs=1))
+        big = ctx.enter_context(tc.tile_pool(name="big", bufs=1))
+        work = ctx.enter_context(tc.tile_pool(name="work", bufs=2))
+        psum = ctx.enter_context(tc.psum_pool(name="psum", bufs=2))
+
+        ident_b = const.tile([P, P], BF16, name="ident_b")
+        make_identity(nc, ident_b[:])
+        ident_f = const.tile([P, P], F32, name="ident_f")
+        make_identity(nc, ident_f[:])
+
+        ctx.enter_context(tc.manual_schedule())
+
+        g_raw = work.tile([P, B, 1024], BF16, name="g_raw", tag="z", bufs=2, align_bytes=64)
+        w1_raw = []
+
+        def load_w1(ch):
+            nk = min(2, K9 - 2 * ch)
+            raw = work.tile([P, 4, 1152], BF16, name="w1_raw%d" % ch, tag="wraw", bufs=3, align_bytes=64)
+            nc.sync.dma_start(out=raw[:, :, 0:nk * 512], in_=w1_v[:, :, ch * 1024:ch * 1024 + nk * 512])
+            w1_raw.append(raw)
+
+        w_raw = []
+
+        def load_w(ch):
+            raw = work.tile([P, 4, 1152], BF16, name="w_raw%d" % ch, tag="wraw", bufs=3, align_bytes=64)
+            nc.sync.dma_start(out=raw[:], in_=w_v[:, :, ch * 1152:(ch + 1) * 1152])
+            w_raw.append(raw)
+
+        z_sb = []
+
+        def load_z(j):
+            zt = work.tile([P, B, 576], F32, name="z%d" % j, tag="z", bufs=2, align_bytes=64)
+            for h in range(2):
+                nc.sync.dma_start(out=zt[:, 4 * h:4 * h + 4, :], in_=z_v[j][:, 4 * h:4 * h + 4, :])
+            z_sb.append(zt)
+
+        def load_g(pr):
+            nc.sync.dma_start(out=g_raw[:, 2 * pr:2 * pr + 2, :], in_=g_v[:, 2 * pr:2 * pr + 2, :])
+
+        for pr in range(3):
+            load_g(pr)
+            load_w1(pr)
+        load_g(3)
+        x_raw = work.tile([P, B, 256], BF16, name="x_raw", tag="ot", bufs=3, align_bytes=64)
+        nc.sync.dma_start(out=x_raw[:], in_=x_v)
+
+        stack = const.tile([P, 32], BF16, name="stack")
+        for r in range(4):
+            rows = slice(32 * r, 32 * r + 32)
+            nc.vector.tensor_copy(out=stack[rows, :], in_=ident_b[rows, rows])
+        base = const.tile([P, K9, 32], BF16, name="base")
+        nc.vector.memset(base[:], 0.0)
+        stack_v = stack[:].rearrange("p (u c) -> p u c", c=8)
+        for s in range(K9):
+            dy, dx = RING[s] if s < 8 else (0, 0)
+            u0, u1 = max(0, dy), min(4, 4 + dy)
+            c0, c1 = max(0, dx), min(8, 8 + dx)
+            dst = base[:, s, :].rearrange("p (u c) -> p u c", c=8)
+            nc.vector.tensor_copy(out=dst[:, u0:u1, c0:c1], in_=stack_v[:, u0 - dy:u1 - dy, c0 - dx:c1 - dx])
+        rot = const.tile([P, K9, 32], BF16, name="rot")
+        for r in range(4):
+            rows = slice(32 * r, 32 * r + 32)
+            nc.vector.tensor_copy(out=rot[rows, 0:8 - 2 * r, :], in_=base[rows, 2 * r:8, :])
+            if r:
+                nc.vector.tensor_copy(out=rot[rows, 8 - 2 * r:8, :], in_=base[rows, 0:2 * r, :])
+        nc.vector.tensor_copy(out=rot[:, 8, :], in_=base[:, 8, :])
+        shift = []
+        for n, (a, u, rn) in enumerate(SETS):
+            sh = const.tile([P, K9, 8 * rn], BF16, name="shift%d" % n)
+            nc.vector.tensor_copy(out=sh[:], in_=rot[:, :, 8 * u:8 * (u + rn)])
+            shift.append(sh)
+
+        gs = []
+        for h in range(2):
+            gst = work.tile([P, 3, 4, 512], BF16, name="gs%d" % h, tag=("z", "stg")[h], bufs=2, align_bytes=64)
+            gs.append(gst)
+
+        def g_sort(pr):
+            h, bl = pr // 2, 2 * (pr % 2)
+            src = g_raw[:, 2 * pr:2 * pr + 2, :].rearrange("p b (m e) -> p (b m) e", e=64)
+            for n, (a, u, rn) in enumerate(SETS):
+                dst = gs[h][:, n, bl:bl + 2, :].rearrange("p b (m e) -> p (b m) e", e=32)
+                nc.vector.tensor_copy(out=dst, in_=src[:, :, 8 * a:8 * a + 32])
+
+        dy = big.tile([P, K9, T, 4], BF16, name="dy", tag="dyz", align_bytes=64)
+        w1_q = []
+        for j in range(4):
+            wc = work.tile([P, K9, P], U32, name="w1_codes%d" % j, tag="wc", bufs=5, align_bytes=64)
+            wsc = work.tile([P, K9, P], U8, name="w1_scales%d" % j, tag="ws", bufs=5, align_bytes=64)
+            w1_q.append((wc, wsc))
+        dy_codes = big.tile([P, K9, T], U32, name="dy_codes", align_bytes=64)
+        dy_scales = big.tile([P, K9, T], U8, name="dy_scales", align_bytes=64)
+        x_codes = big.tile([P, C], U32, name="x_codes", align_bytes=64)
+        x_scales = big.tile([P, C], U8, name="x_scales", align_bytes=64)
+
+        g_t = {}
+
+        def g_transpose(b):
+            gt = work.tile([P, 3, 4, P], BF16, name="gt%d" % b, tag="tg", bufs=2, align_bytes=64)
+            g_t[b] = gt
+            for n in range(3):
+                tp = psum.tile([P, 4, P], BF16, name="gtp%d_%d" % (b, n), tag=("tr", "gw")[(3 * b + n) % 2], bufs=2)
+                for j in range(4):
+                    nc.tensor.transpose(tp[:, j, :], gs[b // 4][:, n, b % 4, j * P:(j + 1) * P], ident_b[:])
+                nc.scalar.copy(out=gt[:, n], in_=tp[:])
+
+        def dy_image(b):
+            for n, (a, u, rn) in enumerate(SETS):
+                nt = 8 * rn
+                dp = psum.tile([P, 4, 256], BF16, name="dyp%d_%d" % (b, n), tag="mm", bufs=4)
+                for j in range(4):
+                    nc.tensor.matmul(out=dp[:, j, 0:K9 * nt], lhsT=g_t[b][:, n, j, :],
+                                     rhs=shift[n][:].rearrange("p k n -> p (k n)"), start=True, stop=True)
+                t0 = 64 * b + 8 * (a + u)
+                nc.scalar.copy(out=dy[:, :, t0:t0 + nt, :],
+                               in_=dp[:, :, 0:K9 * nt].rearrange("p j (k n) -> p k n j", k=K9))
+
+        w1_grp = {}
+
+        def w1_interleave(k):
+            grp = work.tile([P, 2048], BF16, name="w1g%d" % k, tag="wg", bufs=3, align_bytes=64)
+            w1_grp[k] = grp
+            raw = w1_raw[k // 2][:, :, (k % 2) * 512:(k % 2) * 512 + 512]
+            copy = nc.scalar.copy if k in S_W1 else nc.vector.tensor_copy
+            copy(out=grp[:].rearrange("p (j c t) -> p j c t", j=4, t=4),
+                 in_=raw.rearrange("p t (c j) -> p j c t", j=4))
+
+        def w1_quantize(k):
+            for j in range(4):
+                codes, scales = w1_q[j]
+                nc.vector.quantize_mx(out=codes[:, k, :].bitcast(E4M3), scales=scales[:, k, :],
+                                      in_=w1_grp[k][:, 512 * j:512 * j + 512])
+
+        def dy_quantize(k, h):
+            ts = slice(256 * h, 256 * h + 256)
+            nc.vector.quantize_mx(out=dy_codes[:, k, ts].bitcast(E5M2), scales=dy_scales[:, k, ts],
+                                  in_=dy[:, k, ts, :].rearrange("p t j -> p (t j)"))
+
+        def x_prepare():
+            x_sort = work.tile([P, 4, T], BF16, name="x_sort", tag="wg", bufs=3, align_bytes=64)
+            nc.vector.tensor_copy(out=x_sort[:].rearrange("p c (b n) -> p c b n", b=B),
+                                  in_=x_raw[:].rearrange("p b (c n) -> p c b n", c=4))
+            x_grp = work.tile([P, 2048], BF16, name="x_grp", tag="wg", bufs=3, align_bytes=64)
+            x_out = x_grp[:].bitcast(F32).rearrange("p (c t u) -> p c t u", t=4, u=2)
+            for h in range(2):
+                tp = psum.tile([P, 2, 2, P], F32, name="xtp%d" % h, tag="tr", bufs=2)
+                for m in range(2):
+                    words = x_sort[:, 2 * h + m, :].bitcast(F32)
+                    for u in range(2):
+                        nc.tensor.transpose(tp[:, m, u, :], words[:, u:256:2], ident_f[:])
+                nc.scalar.copy(out=x_out[:, :, 2 * h:2 * h + 2, :], in_=tp[:].rearrange("p m u c -> p c m u"))
+            return x_grp
+
+        g_sort(0)
+        for b in range(B + 1):
+            if b < B:
+                g_transpose(b)
+            w1_interleave(b)
+            if b in (1, 3):
+                load_w1(b // 2 + 3)
+            if b in (0, 2, 4):
+                g_sort(b // 2 + 1)
+            if b:
+                w1_quantize(b - 1)
+                dy_image(b - 1)
+            if b == 5:
+                load_z(0)
+            if b == 6:
+                x_grp = x_prepare()
+            if b == 7:
+                nc.vector.quantize_mx(out=x_codes[:].bitcast(E4M3), scales=x_scales[:], in_=x_grp[:])
+                load_w(0)
+                load_w(1)
+                load_z(1)
+        for k in range(K9):
+            dy_quantize(k, 0)
+        w1_quantize(8)
+        load_w(2)
+        for k in range(K9):
+            dy_quantize(k, 1)
+
+        dz = big.tile([P, K9, 4, T], BF16, name="dz", tag="dyz", align_bytes=64)
+        dh_ps, tr_ps, t_grp, t_codes, gw_ps, stg = {}, {}, {}, {}, {}, {}
+
+        def dh_matmul(i):
+            j, k = divmod(i, K9)
+            ps = psum.tile([P, T], F32, name="dh%d" % i, tag="mm", bufs=4)
+            dh_ps[i] = ps
+            codes, scales = w1_q[j]
+            nc.tensor.matmul_mx(out=ps[:], lhsT=codes[:, k, :].bitcast(E4M3), lhsT_scale=scales[:, k, :],
+                                rhs=dy_codes[:, k, :].bitcast(E5M2), rhs_scale=dy_scales[:, k, :],
+                                start=True, stop=True)
+
+        def mask(i):
+            j, k = divmod(i, K9)
+            nc.vector.scalar_tensor_tensor(
+                out=dz[:, k, j, :].rearrange("p (b n) -> p b n", b=B),
+                in0=z_sb[j][:, :, 64 * k:64 * k + 64], scalar=0.0,
+                in1=dh_ps[i][:].rearrange("p (b n) -> p b n", b=B),
+                op0=ALU.is_gt, op1=ALU.mult)
+
+        def dz_transpose(n):
+            tp = psum.tile([P, 2, 2, P], F32, name="trp%d" % n, tag="tr", bufs=2)
+            tr_ps[n] = tp
+            for m in range(2):
+                j, k = divmod(2 * n + m, K9)
+                words = dz[:, k, j, :].bitcast(F32)
+                for u in range(2):
+                    nc.tensor.transpose(tp[:, m, u, :], words[:, u:256:2], ident_f[:])
+
+        def dz_t_copy(n):
+            grp = work.tile([P, 1024], BF16, name="tg%d" % n, tag="tg", bufs=2, align_bytes=64)
+            t_grp[n] = grp
+            (nc.vector.tensor_copy if TENG == "v" else nc.scalar.copy)(
+                out=grp[:].bitcast(F32).rearrange("p (m r u) -> p m r u", m=2, u=2),
+                in_=tr_ps[n][:].rearrange("p m u r -> p m r u"))
+
+        def dz_t_quantize(n):
+            codes = work.tile([P, 256], U32, name="tc%d" % n, tag="tc", bufs=3, align_bytes=64)
+            scales = work.tile([P, 256], U8, name="ts%d" % n, tag="ts", bufs=3, align_bytes=64)
+            t_codes[n] = (codes, scales)
+            nc.vector.quantize_mx(out=codes[:].bitcast(E5M2), scales=scales[:], in_=t_grp[n][:])
+
+        def gw_matmul(i):
+            codes, scales = t_codes[i // 2]
+            cols = slice((i % 2) * P, (i % 2) * P + P)
+            ps = psum.tile([P, C], F32, name="gw%d" % i, tag="gw", bufs=2)
+            gw_ps[i] = ps
+            nc.tensor.matmul_mx(out=ps[:], lhsT=codes[:, cols].bitcast(E5M2), lhsT_scale=scales[:, cols],
+                                rhs=x_codes[:].bitcast(E4M3), rhs_scale=x_scales[:], start=True, stop=True)
+
+        def gw_copy(i, eng):
+            j, k = divmod(i, K9)
+            if k == 0:
+                stage = work.tile([P, K9, C], F32, name="stg%d" % j, tag="stg", bufs=2, align_bytes=64)
+                stg[j] = stage
+            (nc.vector.tensor_copy if eng == "v" else nc.scalar.copy)(out=stg[j][:, k, :], in_=gw_ps[i][:])
+
+        def gw_store(j, cc):
+            ot = work.tile([P, P, K9], F32, name="ot%d_%d" % (j, cc), tag="ot", bufs=3, align_bytes=64)
+            eng = "g" if j < 3 else KLAST[cc]
+            if eng == "s":
+                nc.scalar.copy(out=ot[:], in_=stg[j][:, :, cc * P:(cc + 1) * P].rearrange("p k c -> p c k"))
+            elif eng == "g":
+                nc.gpsimd.tensor_scalar(out=ot[:], in0=stg[j][:, :, cc * P:(cc + 1) * P].rearrange("p k c -> p c k"),
+                                        scalar1=1.0, scalar2=0.0, op0=ALU.mult, op1=ALU.add)
+            else:
+                nc.vector.tensor_copy(out=ot[:], in_=stg[j][:, :, cc * P:(cc + 1) * P].rearrange("p k c -> p c k"))
+            nc.sync.dma_start(out=o1_v[j][:, cc * 1152:(cc + 1) * 1152], in_=ot[:].rearrange("p c k -> p (c k)"))
+
+        w_grp, w_q = {}, []
+        W_PARTS = [(0, 4), (4, 8), (8, 9)]
+
+        def w_interleave(ch, part):
+            k0, k1 = W_PARTS[part]
+            grp = work.tile([P, 2048], BF16, name="wg%d_%d" % (ch, part), tag="wg", bufs=3, align_bytes=64)
+            w_grp[ch, part] = grp
+            nc.scalar.copy(out=grp[:, 0:512 * (k1 - k0)].rearrange("p (k c t) -> p k c t", c=P, t=4),
+                           in_=w_raw[ch][:].rearrange("p t (c k) -> p k c t", k=K9)[:, k0:k1])
+
+        def w_quantize(ch, part):
+            k0, k1 = W_PARTS[part]
+            if part == 0:
+                wc = work.tile([P, K9, P], U32, name="w_codes%d" % ch, tag="wc", bufs=5, align_bytes=64)
+                wsc = work.tile([P, K9, P], U8, name="w_scales%d" % ch, tag="ws", bufs=5, align_bytes=64)
+                w_q.append((wc, wsc))
+            codes, scales = w_q[ch]
+            nc.vector.quantize_mx(out=codes[:, k0:k1, :].rearrange("p k c -> p (k c)").bitcast(E4M3),
+                                  scales=scales[:, k0:k1, :].rearrange("p k c -> p (k c)"),
+                                  in_=w_grp[ch, part][:, 0:512 * (k1 - k0)])
+
+        m_grp, m_codes = {}, {}
+
+        def dz_m_interleave(k, eng):
+            grp = work.tile([P, 2048], BF16, name="mg%d" % k, tag="wg", bufs=3, align_bytes=64)
+            m_grp[k] = grp
+            dst = grp[:].rearrange("p (c i t) -> p c t i", i=4, t=4)
+            src = dz[:, k].rearrange("p t (c i) -> p c t i", i=4)
+            if eng == "v":
+                nc.vector.tensor_copy(out=dst, in_=src)
+            else:
+                nc.scalar.copy(out=dst, in_=src)
+
+        def dz_m_quantize(k):
+            codes = work.tile([P, T], U32, name="mc%d" % k, tag="mc", bufs=4, align_bytes=64)
+            scales = work.tile([P, T], U8, name="ms%d" % k, tag="ms", bufs=4, align_bytes=64)
+            m_codes[k] = (codes, scales)
+            nc.vector.quantize_mx(out=codes[:].bitcast(E5M2), scales=scales[:], in_=m_grp[k][:])
+
+        gx_ps = []
+
+        def gx_matmul(k):
+            codes, scales = m_codes[k]
+            for ch in range(4):
+                if k == 0:
+                    gxp = psum.tile([P, T], F32, name="gx%d" % ch, tag="mm", bufs=4)
+                    gx_ps.append(gxp)
+                nc.tensor.matmul_mx(out=gx_ps[ch][:], lhsT=w_q[ch][0][:, k, :].bitcast(E4M3),
+                                    lhsT_scale=w_q[ch][1][:, k, :], rhs=codes[:].bitcast(E5M2), rhs_scale=scales[:],
+                                    start=(k == 0), stop=(k == K9 - 1))
+
+        dh_matmul(0)
+        dh_matmul(1)
+        W_AT = {n + 1: (n // 3, n % 3) for n in range(12)}
+        V_GW = (0, 1)
+        todo = []
+        for n in range(STEPS + 2):
+            if n < STEPS:
+                mask(2 * n)
+                if 2 * n % K9 == 8 and 2 * n // K9 < 2:
+                    load_z(2 * n // K9 + 2)
+            if 1 <= n <= STEPS:
+                dz_t_copy(n - 1)
+            if n == STEPS:
+                dz_m_interleave(2, "v")
+            if n < STEPS:
+                mask(2 * n + 1)
+                if (2 * n + 1) % K9 == 8 and (2 * n + 1) // K9 < 2:
+                    load_z((2 * n + 1) // K9 + 2)
+                for i in (2 * n + 2, 2 * n + 3):
+                    if i < 36:
+                        dh_matmul(i)
+            if 1 <= n <= STEPS:
+                dz_t_quantize(n - 1)
+            if n < STEPS:
+                dz_transpose(n)
+            if n in (15, 17):
+                dz_m_quantize((n - 15) // 2)
+            if todo:
+                gw_store(*todo.pop(0))
+            if 2 <= n <= STEPS + 1:
+                for i in (2 * n - 4, 2 * n - 3):
+                    gw_copy(i, "v" if i % 2 and n in W_AT and W_AT[n][1] in V_GW else "s")
+                    if i % K9 == K9 - 1:
+                        todo += [(i // K9, cc) for cc in range(4)]
+            if 1 <= n <= STEPS:
+                gw_matmul(2 * n - 2)
+                gw_matmul(2 * n - 1)
+            if n in W_AT:
+                ch, part = W_AT[n]
+                w_interleave(ch, part)
+                if ch == 0 and part == 2:
+                    load_w(3)
+            if n - 1 in W_AT:
+                w_quantize(*W_AT[n - 1])
+            if n in (14, 16):
+                dz_m_interleave((n - 14) // 2, "s")
+            if n == STEPS:
+                dz_m_interleave(3, "s")
+                dz_m_quantize(2)
+        gx_matmul(0)
+        gx_matmul(1)
+        gx_matmul(2)
+        gw_store(*todo.pop(0))
+        dz_m_interleave(4, "v")
+        dz_m_quantize(3)
+        gw_store(*todo.pop(0))
+        gw_store(*todo.pop(0))
+        dz_m_quantize(4)
+        gx_matmul(3)
+        dz_m_interleave(5, "v")
+        gw_store(*todo.pop(0))
+        gx_matmul(4)
+        dz_m_quantize(5)
+        dz_m_interleave(6, "s")
+        dz_m_interleave(7, "v")
+        gx_matmul(5)
+        dz_m_interleave(8, "s")
+        dz_m_quantize(6)
+        dz_m_quantize(7)
+        gx_matmul(6)
+        gx_matmul(7)
+        dz_m_quantize(8)
+        gx_matmul(8)
+        for ch in range(4):
+            ot = work.tile([P, B, S * S], F32, name="o0_%d" % ch, tag="ot", bufs=3, align_bytes=64)
+            dst = ot[:].rearrange("p b n -> p (b n)")
+            if ch % 2:
+                nc.vector.tensor_copy(out=dst, in_=gx_ps[ch][:])
+            else:
+                nc.scalar.copy(out=dst, in_=gx_ps[ch][:])
+            nc.sync.dma_start(out=o0_v[ch], in_=ot[:])

@@ -19,8 +19,14 @@ RING = [(-1, -1), (-1, 0), (-1, 1), (0, 1), (1, 1), (1, 0), (1, -1), (0, -1)]
 SETS = [(0, 0, 3), (2, 1, 2), (4, 1, 3)]
 STEPS = 18
 S_W1 = ()
-KLAST = "vvsv"
-TENG = "v"
+W_HEAD = 2
+W_FROM = 0
+V_GW = tuple(range(1, 14, 2))
+M_I = ()
+M_Q = ()
+TAIL = "s0 v1 k s2 q1 k q0 x1 x0 v3 s4 k q2 x2 q3 x3 k v5 q4 x4 s6 q5 x5 v7 s8 q6 x6 q7 x7 q8 x8".split()
+KLAST = {(j, cc): "s" if j == 3 and cc == 3 else "v" for j in range(4) for cc in range(4)}
+TENG = "s"
 
 
 def tile_psr4convf_v_kernel(tc, x, W, W1, z, grad_out, out_0, out_1):
@@ -50,9 +56,9 @@ def tile_psr4convf_v_kernel(tc, x, W, W1, z, grad_out, out_0, out_1):
         w1_raw = []
 
         def load_w1(ch):
-            nk = min(2, K9 - 2 * ch)
+            k0, nk = max(0, 2 * ch - 1), min(2, 2 * ch + 1)
             raw = work.tile([P, 4, 1152], BF16, name="w1_raw%d" % ch, tag="wraw", bufs=3, align_bytes=64)
-            nc.sync.dma_start(out=raw[:, :, 0:nk * 512], in_=w1_v[:, :, ch * 1024:ch * 1024 + nk * 512])
+            nc.sync.dma_start(out=raw[:, :, 0:nk * 512], in_=w1_v[:, :, 512 * k0:512 * (k0 + nk)])
             w1_raw.append(raw)
 
         w_raw = []
@@ -154,12 +160,14 @@ def tile_psr4convf_v_kernel(tc, x, W, W1, z, grad_out, out_0, out_1):
         w1_grp = {}
 
         def w1_interleave(k):
-            grp = work.tile([P, 2048], BF16, name="w1g%d" % k, tag="wg", bufs=3, align_bytes=64)
+            grp = work.tile([P, 2048], BF16, name="w1g%d" % k, tag="wg", bufs=4, align_bytes=64)
             w1_grp[k] = grp
-            raw = w1_raw[k // 2][:, :, (k % 2) * 512:(k % 2) * 512 + 512]
-            copy = nc.scalar.copy if k in S_W1 else nc.vector.tensor_copy
-            copy(out=grp[:].rearrange("p (j c t) -> p j c t", j=4, t=4),
-                 in_=raw.rearrange("p t (c j) -> p j c t", j=4))
+            part = (k + 1) // 2
+            k_in = k - max(0, 2 * part - 1)
+            raw = w1_raw[part][:, :, 512 * k_in:512 * k_in + 512]
+            nc.vector.tensor_copy(
+                 out=grp[:].rearrange("p (j c t) -> p c t j", j=4, t=4),
+                 in_=raw.rearrange("p t (c j) -> p c t j", j=4))
 
         def w1_quantize(k):
             for j in range(4):
@@ -173,10 +181,10 @@ def tile_psr4convf_v_kernel(tc, x, W, W1, z, grad_out, out_0, out_1):
                                   in_=dy[:, k, ts, :].rearrange("p t j -> p (t j)"))
 
         def x_prepare():
-            x_sort = work.tile([P, 4, T], BF16, name="x_sort", tag="wg", bufs=3, align_bytes=64)
+            x_sort = work.tile([P, 4, T], BF16, name="x_sort", tag="wg", bufs=4, align_bytes=64)
             nc.vector.tensor_copy(out=x_sort[:].rearrange("p c (b n) -> p c b n", b=B),
                                   in_=x_raw[:].rearrange("p b (c n) -> p c b n", c=4))
-            x_grp = work.tile([P, 2048], BF16, name="x_grp", tag="wg", bufs=3, align_bytes=64)
+            x_grp = work.tile([P, 2048], BF16, name="x_grp", tag="wg", bufs=4, align_bytes=64)
             x_out = x_grp[:].bitcast(F32).rearrange("p (c t u) -> p c t u", t=4, u=2)
             for h in range(2):
                 tp = psum.tile([P, 2, 2, P], F32, name="xtp%d" % h, tag="tr", bufs=2)
@@ -192,7 +200,7 @@ def tile_psr4convf_v_kernel(tc, x, W, W1, z, grad_out, out_0, out_1):
             if b < B:
                 g_transpose(b)
             w1_interleave(b)
-            if b in (1, 3):
+            if b in (0, 2):
                 load_w1(b // 2 + 3)
             if b in (0, 2, 4):
                 g_sort(b // 2 + 1)
@@ -204,13 +212,13 @@ def tile_psr4convf_v_kernel(tc, x, W, W1, z, grad_out, out_0, out_1):
             if b == 6:
                 x_grp = x_prepare()
             if b == 7:
-                nc.vector.quantize_mx(out=x_codes[:].bitcast(E4M3), scales=x_scales[:], in_=x_grp[:])
                 load_w(0)
                 load_w(1)
                 load_z(1)
         for k in range(K9):
             dy_quantize(k, 0)
         w1_quantize(8)
+        nc.vector.quantize_mx(out=x_codes[:].bitcast(E4M3), scales=x_scales[:], in_=x_grp[:])
         load_w(2)
         for k in range(K9):
             dy_quantize(k, 1)
@@ -274,7 +282,7 @@ def tile_psr4convf_v_kernel(tc, x, W, W1, z, grad_out, out_0, out_1):
 
         def gw_store(j, cc):
             ot = work.tile([P, P, K9], F32, name="ot%d_%d" % (j, cc), tag="ot", bufs=3, align_bytes=64)
-            eng = "g" if j < 3 else KLAST[cc]
+            eng = KLAST[(j, cc)]
             if eng == "s":
                 nc.scalar.copy(out=ot[:], in_=stg[j][:, :, cc * P:(cc + 1) * P].rearrange("p k c -> p c k"))
             elif eng == "g":
@@ -284,31 +292,32 @@ def tile_psr4convf_v_kernel(tc, x, W, W1, z, grad_out, out_0, out_1):
                 nc.vector.tensor_copy(out=ot[:], in_=stg[j][:, :, cc * P:(cc + 1) * P].rearrange("p k c -> p c k"))
             nc.sync.dma_start(out=o1_v[j][:, cc * 1152:(cc + 1) * 1152], in_=ot[:].rearrange("p c k -> p (c k)"))
 
-        w_grp, w_q = {}, []
-        W_PARTS = [(0, 4), (4, 8), (8, 9)]
+        w_grp, w_q = {}, {}
+        W_PARTS = [(ch, k, min(k + 2, K9)) for ch in range(4) for k in range(0, K9, 2)]
 
-        def w_interleave(ch, part):
-            k0, k1 = W_PARTS[part]
-            grp = work.tile([P, 2048], BF16, name="wg%d_%d" % (ch, part), tag="wg", bufs=3, align_bytes=64)
-            w_grp[ch, part] = grp
-            nc.scalar.copy(out=grp[:, 0:512 * (k1 - k0)].rearrange("p (k c t) -> p k c t", c=P, t=4),
-                           in_=w_raw[ch][:].rearrange("p t (c k) -> p k c t", k=K9)[:, k0:k1])
+        def w_interleave(part):
+            ch, k0, k1 = W_PARTS[part]
+            nk = k1 - k0
+            grp = work.tile([P, 2048], BF16, name="wg%d" % part, tag="wg", bufs=4, align_bytes=64)
+            w_grp[part] = grp
+            nc.scalar.copy(out=grp[:, 0:512 * nk].rearrange("p (k c t) -> p c t k", c=P, t=4),
+                           in_=w_raw[ch][:].rearrange("p t (c k) -> p c t k", k=K9)[:, :, :, k0:k1])
 
-        def w_quantize(ch, part):
-            k0, k1 = W_PARTS[part]
-            if part == 0:
+        def w_quantize(part):
+            ch, k0, k1 = W_PARTS[part]
+            if k0 == 0:
                 wc = work.tile([P, K9, P], U32, name="w_codes%d" % ch, tag="wc", bufs=5, align_bytes=64)
                 wsc = work.tile([P, K9, P], U8, name="w_scales%d" % ch, tag="ws", bufs=5, align_bytes=64)
-                w_q.append((wc, wsc))
+                w_q[ch] = (wc, wsc)
             codes, scales = w_q[ch]
             nc.vector.quantize_mx(out=codes[:, k0:k1, :].rearrange("p k c -> p (k c)").bitcast(E4M3),
                                   scales=scales[:, k0:k1, :].rearrange("p k c -> p (k c)"),
-                                  in_=w_grp[ch, part][:, 0:512 * (k1 - k0)])
+                                  in_=w_grp[part][:, 0:512 * (k1 - k0)])
 
         m_grp, m_codes = {}, {}
 
         def dz_m_interleave(k, eng):
-            grp = work.tile([P, 2048], BF16, name="mg%d" % k, tag="wg", bufs=3, align_bytes=64)
+            grp = work.tile([P, 2048], BF16, name="mg%d" % k, tag="wg", bufs=4, align_bytes=64)
             m_grp[k] = grp
             dst = grp[:].rearrange("p (c i t) -> p c t i", i=4, t=4)
             src = dz[:, k].rearrange("p t (c i) -> p c t i", i=4)
@@ -318,101 +327,88 @@ def tile_psr4convf_v_kernel(tc, x, W, W1, z, grad_out, out_0, out_1):
                 nc.scalar.copy(out=dst, in_=src)
 
         def dz_m_quantize(k):
-            codes = work.tile([P, T], U32, name="mc%d" % k, tag="mc", bufs=4, align_bytes=64)
-            scales = work.tile([P, T], U8, name="ms%d" % k, tag="ms", bufs=4, align_bytes=64)
+            codes = work.tile([P, T], U32, name="mc%d" % k, tag="mc", bufs=3, align_bytes=64)
+            scales = work.tile([P, T], U8, name="ms%d" % k, tag="ms", bufs=3, align_bytes=64)
             m_codes[k] = (codes, scales)
             nc.vector.quantize_mx(out=codes[:].bitcast(E5M2), scales=scales[:], in_=m_grp[k][:])
 
-        gx_ps = []
+        gx_ps, gx_seen = [], []
 
         def gx_matmul(k):
             codes, scales = m_codes[k]
+            gx_seen.append(k)
             for ch in range(4):
-                if k == 0:
+                if len(gx_seen) == 1:
                     gxp = psum.tile([P, T], F32, name="gx%d" % ch, tag="mm", bufs=4)
                     gx_ps.append(gxp)
                 nc.tensor.matmul_mx(out=gx_ps[ch][:], lhsT=w_q[ch][0][:, k, :].bitcast(E4M3),
                                     lhsT_scale=w_q[ch][1][:, k, :], rhs=codes[:].bitcast(E5M2), rhs_scale=scales[:],
-                                    start=(k == 0), stop=(k == K9 - 1))
+                                    start=(len(gx_seen) == 1), stop=(len(gx_seen) == K9))
 
         dh_matmul(0)
         dh_matmul(1)
-        W_AT = {n + 1: (n // 3, n % 3) for n in range(12)}
-        V_GW = (0, 1)
         todo = []
+        next_w = 0
+        for part in range(W_HEAD):
+            w_interleave(part)
+        w_done = 0
+        w_next = W_HEAD
         for n in range(STEPS + 2):
             if n < STEPS:
                 mask(2 * n)
-                if 2 * n % K9 == 8 and 2 * n // K9 < 2:
-                    load_z(2 * n // K9 + 2)
-            if 1 <= n <= STEPS:
-                dz_t_copy(n - 1)
-            if n == STEPS:
-                dz_m_interleave(2, "v")
-            if n < STEPS:
                 mask(2 * n + 1)
-                if (2 * n + 1) % K9 == 8 and (2 * n + 1) // K9 < 2:
-                    load_z((2 * n + 1) // K9 + 2)
+                for i in (2 * n, 2 * n + 1):
+                    if i in (8, 17):
+                        load_z(i // K9 + 2)
                 for i in (2 * n + 2, 2 * n + 3):
                     if i < 36:
                         dh_matmul(i)
             if 1 <= n <= STEPS:
+                dz_t_copy(n - 1)
+            if w_done < w_next:
+                w_quantize(w_done)
+                w_done += 1
+            if todo:
+                gw_store(*todo.pop(0))
+            if 1 <= n <= STEPS:
                 dz_t_quantize(n - 1)
             if n < STEPS:
                 dz_transpose(n)
-            if n in (15, 17):
-                dz_m_quantize((n - 15) // 2)
-            if todo:
-                gw_store(*todo.pop(0))
+            for k, q in M_Q:
+                if q == n:
+                    dz_m_quantize(k)
             if 2 <= n <= STEPS + 1:
                 for i in (2 * n - 4, 2 * n - 3):
-                    gw_copy(i, "v" if i % 2 and n in W_AT and W_AT[n][1] in V_GW else "s")
+                    gw_copy(i, "v" if i in V_GW else "s")
                     if i % K9 == K9 - 1:
                         todo += [(i // K9, cc) for cc in range(4)]
             if 1 <= n <= STEPS:
                 gw_matmul(2 * n - 2)
                 gw_matmul(2 * n - 1)
-            if n in W_AT:
-                ch, part = W_AT[n]
-                w_interleave(ch, part)
-                if ch == 0 and part == 2:
+            if w_next < 20 and n >= W_FROM:
+                w_interleave(w_next)
+                w_next += 1
+                if w_next == 6:
                     load_w(3)
-            if n - 1 in W_AT:
-                w_quantize(*W_AT[n - 1])
-            if n in (14, 16):
-                dz_m_interleave((n - 14) // 2, "s")
-            if n == STEPS:
-                dz_m_interleave(3, "s")
-                dz_m_quantize(2)
-        gx_matmul(0)
-        gx_matmul(1)
-        gx_matmul(2)
-        gw_store(*todo.pop(0))
-        dz_m_interleave(4, "v")
-        dz_m_quantize(3)
-        gw_store(*todo.pop(0))
-        gw_store(*todo.pop(0))
-        dz_m_quantize(4)
-        gx_matmul(3)
-        dz_m_interleave(5, "v")
-        gw_store(*todo.pop(0))
-        gx_matmul(4)
-        dz_m_quantize(5)
-        dz_m_interleave(6, "s")
-        dz_m_interleave(7, "v")
-        gx_matmul(5)
-        dz_m_interleave(8, "s")
-        dz_m_quantize(6)
-        dz_m_quantize(7)
-        gx_matmul(6)
-        gx_matmul(7)
-        dz_m_quantize(8)
-        gx_matmul(8)
-        for ch in range(4):
-            ot = work.tile([P, B, S * S], F32, name="o0_%d" % ch, tag="ot", bufs=3, align_bytes=64)
-            dst = ot[:].rearrange("p b n -> p (b n)")
-            if ch % 2:
-                nc.vector.tensor_copy(out=dst, in_=gx_ps[ch][:])
+            for k, e, q in M_I:
+                if q == n:
+                    dz_m_interleave(k, e)
+        while w_done < w_next:
+            w_quantize(w_done)
+            w_done += 1
+        for item in TAIL:
+            if item == "k":
+                gw_store(*todo.pop(0))
+            elif item[0] == "x":
+                gx_matmul(int(item[1]))
+            elif item[0] == "q":
+                dz_m_quantize(int(item[1]))
             else:
-                nc.scalar.copy(out=dst, in_=gx_ps[ch][:])
-            nc.sync.dma_start(out=o0_v[ch], in_=ot[:])
+                dz_m_interleave(int(item[1]), item[0])
+        gx_out = work.tile([P, 4, T], F32, name="gx_out", tag="stg", bufs=2, align_bytes=64)
+        for ch in range(4):
+            if ch % 2:
+                nc.vector.tensor_copy(out=gx_out[:, ch, :], in_=gx_ps[ch][:])
+            else:
+                nc.scalar.copy(out=gx_out[:, ch, :], in_=gx_ps[ch][:])
+            nc.sync.dma_start(out=o0_v[ch], in_=gx_out[:, ch, :].rearrange("p (b n) -> p b n", b=B))

@@ -19,20 +19,33 @@ RING = [(-1, -1), (-1, 0), (-1, 1), (0, 1), (1, 1), (1, 0), (1, -1), (0, -1)]
 SETS = [(0, 0, 3), (2, 1, 2), (4, 1, 3)]
 STEPS = 18
 S_W1 = ()
-W_HEAD = 2
+G_W = ()
+V_W = tuple(range(2, 20, 3))
+V_DY = ()
+W_LAG = 2
+LQ = 1
+DHA = 2
+MMB = 4
+TRB = 2
+GWB = 2
+TGB = 2
+WGB = 4
+TCB = 3
+W_HEAD_Q = 0
+W_HEAD = 3
 W_FROM = 0
-V_GW = tuple(range(1, 14, 2))
+V_GW = ()
 M_I = ()
 M_Q = ()
 TAIL = "s0 v1 k s2 q1 k q0 x1 x0 v3 s4 k q2 x2 q3 x3 k v5 q4 x4 s6 q5 x5 v7 s8 q6 x6 q7 x7 q8 x8".split()
-KLAST = {(j, cc): "s" if j == 3 and cc == 3 else "v" for j in range(4) for cc in range(4)}
+KLAST = {(j, cc): "v" for j in range(4) for cc in range(4)}
 TENG = "s"
 
 
 def tile_psr4convf_v_kernel(tc, x, W, W1, z, grad_out, out_0, out_1):
     nc = tc.nc
     g_v = grad_out.rearrange("b (q j) r h w -> q b (j r h w)", j=4)
-    x_v = x.rearrange("b (p c) h w -> p b (c h w)", c=4)
+    x_v = x.rearrange("b (c p) h w -> c p b (h w)", p=P)
     w1_v = W1.rearrange("(p j) m -> p j m", j=4)
     w_v = W.rearrange("(p j) c k -> p j (c k)", j=4)
     z_v = z.rearrange("b (p j) k h w -> j p b (k h w)", j=4)
@@ -83,15 +96,16 @@ def tile_psr4convf_v_kernel(tc, x, W, W1, z, grad_out, out_0, out_1):
             load_g(pr)
             load_w1(pr)
         load_g(3)
-        x_raw = work.tile([P, B, 256], BF16, name="x_raw", tag="ot", bufs=3, align_bytes=64)
-        nc.sync.dma_start(out=x_raw[:], in_=x_v)
+        x_raw = work.tile([P, 4, T], BF16, name="x_raw", tag="ot", bufs=3, align_bytes=64)
+        for ct in range(4):
+            nc.sync.dma_start(out=x_raw[:, ct, :].rearrange("p (b n) -> p b n", b=B), in_=x_v[ct])
 
+        base = const.tile([P, K9, 32], BF16, name="base")
+        nc.vector.memset(base[:], 0.0)
         stack = const.tile([P, 32], BF16, name="stack")
         for r in range(4):
             rows = slice(32 * r, 32 * r + 32)
             nc.vector.tensor_copy(out=stack[rows, :], in_=ident_b[rows, rows])
-        base = const.tile([P, K9, 32], BF16, name="base")
-        nc.vector.memset(base[:], 0.0)
         stack_v = stack[:].rearrange("p (u c) -> p u c", c=8)
         for s in range(K9):
             dy, dx = RING[s] if s < 8 else (0, 0)
@@ -138,10 +152,10 @@ def tile_psr4convf_v_kernel(tc, x, W, W1, z, grad_out, out_0, out_1):
         g_t = {}
 
         def g_transpose(b):
-            gt = work.tile([P, 3, 4, P], BF16, name="gt%d" % b, tag="tg", bufs=2, align_bytes=64)
+            gt = work.tile([P, 3, 4, P], BF16, name="gt%d" % b, tag="tg", bufs=TGB, align_bytes=64)
             g_t[b] = gt
             for n in range(3):
-                tp = psum.tile([P, 4, P], BF16, name="gtp%d_%d" % (b, n), tag=("tr", "gw")[(3 * b + n) % 2], bufs=2)
+                tp = psum.tile([P, 4, P], BF16, name="gtp%d_%d" % (b, n), tag=("tr", "gw")[(3 * b + n) % 2], bufs=(TRB, GWB)[(3 * b + n) % 2])
                 for j in range(4):
                     nc.tensor.transpose(tp[:, j, :], gs[b // 4][:, n, b % 4, j * P:(j + 1) * P], ident_b[:])
                 nc.scalar.copy(out=gt[:, n], in_=tp[:])
@@ -149,25 +163,26 @@ def tile_psr4convf_v_kernel(tc, x, W, W1, z, grad_out, out_0, out_1):
         def dy_image(b):
             for n, (a, u, rn) in enumerate(SETS):
                 nt = 8 * rn
-                dp = psum.tile([P, 4, 256], BF16, name="dyp%d_%d" % (b, n), tag="mm", bufs=4)
+                dp = psum.tile([P, 4, 256], BF16, name="dyp%d_%d" % (b, n), tag="mm", bufs=MMB)
                 for j in range(4):
                     nc.tensor.matmul(out=dp[:, j, 0:K9 * nt], lhsT=g_t[b][:, n, j, :],
                                      rhs=shift[n][:].rearrange("p k n -> p (k n)"), start=True, stop=True)
                 t0 = 64 * b + 8 * (a + u)
-                nc.scalar.copy(out=dy[:, :, t0:t0 + nt, :],
+                copy = nc.vector.tensor_copy if (b, n) in V_DY else nc.scalar.copy
+                copy(out=dy[:, :, t0:t0 + nt, :],
                                in_=dp[:, :, 0:K9 * nt].rearrange("p j (k n) -> p k n j", k=K9))
 
         w1_grp = {}
 
         def w1_interleave(k):
-            grp = work.tile([P, 2048], BF16, name="w1g%d" % k, tag="wg", bufs=4, align_bytes=64)
+            grp = work.tile([P, 2048], BF16, name="w1g%d" % k, tag="wg", bufs=WGB, align_bytes=64)
             w1_grp[k] = grp
             part = (k + 1) // 2
             k_in = k - max(0, 2 * part - 1)
             raw = w1_raw[part][:, :, 512 * k_in:512 * k_in + 512]
             nc.vector.tensor_copy(
-                 out=grp[:].rearrange("p (j c t) -> p c t j", j=4, t=4),
-                 in_=raw.rearrange("p t (c j) -> p c t j", j=4))
+                 out=grp[:].rearrange("p (j n i t) -> p j n t i", j=4, i=2, t=4),
+                 in_=raw.rearrange("p t (n i j) -> p j n t i", i=2, j=4))
 
         def w1_quantize(k):
             for j in range(4):
@@ -180,19 +195,45 @@ def tile_psr4convf_v_kernel(tc, x, W, W1, z, grad_out, out_0, out_1):
             nc.vector.quantize_mx(out=dy_codes[:, k, ts].bitcast(E5M2), scales=dy_scales[:, k, ts],
                                   in_=dy[:, k, ts, :].rearrange("p t j -> p (t j)"))
 
+        w_grp, w_q = {}, {}
+        W_PARTS = [(ch, k, min(k + 2, K9)) for ch in range(4) for k in range(0, K9, 2)]
+
+        def w_interleave(part):
+            ch, k0, k1 = W_PARTS[part]
+            nk = k1 - k0
+            grp = work.tile([P, 2048], BF16, name="wg%d" % part, tag="wg", bufs=WGB, align_bytes=64)
+            w_grp[part] = grp
+            dst = grp[:, 0:512 * nk].rearrange("p (k c t) -> p c t k", c=P, t=4)
+            src = w_raw[ch][:].rearrange("p t (c k) -> p c t k", k=K9)[:, :, :, k0:k1]
+            if part in G_W:
+                nc.gpsimd.tensor_scalar(out=dst, in0=src, scalar1=1.0, scalar2=0.0, op0=ALU.mult, op1=ALU.add)
+            elif part in V_W:
+                nc.vector.tensor_copy(out=dst, in_=src)
+            else:
+                nc.scalar.copy(out=dst, in_=src)
+
+        def w_quantize(part):
+            ch, k0, k1 = W_PARTS[part]
+            if k0 == 0:
+                wc = work.tile([P, K9, P], U32, name="w_codes%d" % ch, tag="wc", bufs=5, align_bytes=64)
+                wsc = work.tile([P, K9, P], U8, name="w_scales%d" % ch, tag="ws", bufs=5, align_bytes=64)
+                w_q[ch] = (wc, wsc)
+            codes, scales = w_q[ch]
+            nc.vector.quantize_mx(out=codes[:, k0:k1, :].rearrange("p k c -> p (k c)").bitcast(E4M3),
+                                  scales=scales[:, k0:k1, :].rearrange("p k c -> p (k c)"),
+                                  in_=w_grp[part][:, 0:512 * (k1 - k0)])
+
         def x_prepare():
-            x_sort = work.tile([P, 4, T], BF16, name="x_sort", tag="wg", bufs=4, align_bytes=64)
-            nc.vector.tensor_copy(out=x_sort[:].rearrange("p c (b n) -> p c b n", b=B),
-                                  in_=x_raw[:].rearrange("p b (c n) -> p c b n", c=4))
-            x_grp = work.tile([P, 2048], BF16, name="x_grp", tag="wg", bufs=4, align_bytes=64)
-            x_out = x_grp[:].bitcast(F32).rearrange("p (c t u) -> p c t u", t=4, u=2)
+            x_grp = work.tile([P, 2048], BF16, name="x_grp", tag="wg", bufs=WGB, align_bytes=64)
+            x_out = x_grp[:].bitcast(F32).rearrange("p (m n i u) -> p m n i u", m=4, i=2, u=2)
             for h in range(2):
-                tp = psum.tile([P, 2, 2, P], F32, name="xtp%d" % h, tag="tr", bufs=2)
+                tp = psum.tile([P, 2, 2, P], F32, name="xtp%d" % h, tag="tr", bufs=TRB)
                 for m in range(2):
-                    words = x_sort[:, 2 * h + m, :].bitcast(F32)
+                    words = x_raw[:, 2 * h + m, :].bitcast(F32)
                     for u in range(2):
                         nc.tensor.transpose(tp[:, m, u, :], words[:, u:256:2], ident_f[:])
-                nc.scalar.copy(out=x_out[:, :, 2 * h:2 * h + 2, :], in_=tp[:].rearrange("p m u c -> p c m u"))
+                for m in range(2):
+                    nc.vector.tensor_copy(out=x_out[:, 2 * h + m], in_=tp[:, m].rearrange("p u (i n) -> p n i u", i=2))
             return x_grp
 
         g_sort(0)
@@ -206,11 +247,10 @@ def tile_psr4convf_v_kernel(tc, x, W, W1, z, grad_out, out_0, out_1):
                 g_sort(b // 2 + 1)
             if b:
                 w1_quantize(b - 1)
+            if b:
                 dy_image(b - 1)
             if b == 5:
                 load_z(0)
-            if b == 6:
-                x_grp = x_prepare()
             if b == 7:
                 load_w(0)
                 load_w(1)
@@ -218,8 +258,13 @@ def tile_psr4convf_v_kernel(tc, x, W, W1, z, grad_out, out_0, out_1):
         for k in range(K9):
             dy_quantize(k, 0)
         w1_quantize(8)
+        x_grp = x_prepare()
         nc.vector.quantize_mx(out=x_codes[:].bitcast(E4M3), scales=x_scales[:], in_=x_grp[:])
         load_w(2)
+        for part in range(W_HEAD):
+            w_interleave(part)
+        for part in range(W_HEAD_Q):
+            w_quantize(part)
         for k in range(K9):
             dy_quantize(k, 1)
 
@@ -228,7 +273,7 @@ def tile_psr4convf_v_kernel(tc, x, W, W1, z, grad_out, out_0, out_1):
 
         def dh_matmul(i):
             j, k = divmod(i, K9)
-            ps = psum.tile([P, T], F32, name="dh%d" % i, tag="mm", bufs=4)
+            ps = psum.tile([P, T], F32, name="dh%d" % i, tag="mm", bufs=MMB)
             dh_ps[i] = ps
             codes, scales = w1_q[j]
             nc.tensor.matmul_mx(out=ps[:], lhsT=codes[:, k, :].bitcast(E4M3), lhsT_scale=scales[:, k, :],
@@ -244,7 +289,7 @@ def tile_psr4convf_v_kernel(tc, x, W, W1, z, grad_out, out_0, out_1):
                 op0=ALU.is_gt, op1=ALU.mult)
 
         def dz_transpose(n):
-            tp = psum.tile([P, 2, 2, P], F32, name="trp%d" % n, tag="tr", bufs=2)
+            tp = psum.tile([P, 2, 2, P], F32, name="trp%d" % n, tag="tr", bufs=TRB)
             tr_ps[n] = tp
             for m in range(2):
                 j, k = divmod(2 * n + m, K9)
@@ -253,22 +298,22 @@ def tile_psr4convf_v_kernel(tc, x, W, W1, z, grad_out, out_0, out_1):
                     nc.tensor.transpose(tp[:, m, u, :], words[:, u:256:2], ident_f[:])
 
         def dz_t_copy(n):
-            grp = work.tile([P, 1024], BF16, name="tg%d" % n, tag="tg", bufs=2, align_bytes=64)
+            grp = work.tile([P, 1024], BF16, name="tg%d" % n, tag="tg", bufs=TGB, align_bytes=64)
             t_grp[n] = grp
             (nc.vector.tensor_copy if TENG == "v" else nc.scalar.copy)(
                 out=grp[:].bitcast(F32).rearrange("p (m r u) -> p m r u", m=2, u=2),
                 in_=tr_ps[n][:].rearrange("p m u r -> p m r u"))
 
         def dz_t_quantize(n):
-            codes = work.tile([P, 256], U32, name="tc%d" % n, tag="tc", bufs=3, align_bytes=64)
-            scales = work.tile([P, 256], U8, name="ts%d" % n, tag="ts", bufs=3, align_bytes=64)
+            codes = work.tile([P, 256], U32, name="tc%d" % n, tag="tc", bufs=TCB, align_bytes=64)
+            scales = work.tile([P, 256], U8, name="ts%d" % n, tag="ts", bufs=TCB, align_bytes=64)
             t_codes[n] = (codes, scales)
             nc.vector.quantize_mx(out=codes[:].bitcast(E5M2), scales=scales[:], in_=t_grp[n][:])
 
         def gw_matmul(i):
             codes, scales = t_codes[i // 2]
             cols = slice((i % 2) * P, (i % 2) * P + P)
-            ps = psum.tile([P, C], F32, name="gw%d" % i, tag="gw", bufs=2)
+            ps = psum.tile([P, C], F32, name="gw%d" % i, tag="gw", bufs=GWB)
             gw_ps[i] = ps
             nc.tensor.matmul_mx(out=ps[:], lhsT=codes[:, cols].bitcast(E5M2), lhsT_scale=scales[:, cols],
                                 rhs=x_codes[:].bitcast(E4M3), rhs_scale=x_scales[:], start=True, stop=True)
@@ -282,42 +327,21 @@ def tile_psr4convf_v_kernel(tc, x, W, W1, z, grad_out, out_0, out_1):
 
         def gw_store(j, cc):
             ot = work.tile([P, P, K9], F32, name="ot%d_%d" % (j, cc), tag="ot", bufs=3, align_bytes=64)
+            ot_v = ot[:].rearrange("p (i n) k -> p n k i", i=2)
             eng = KLAST[(j, cc)]
             if eng == "s":
-                nc.scalar.copy(out=ot[:], in_=stg[j][:, :, cc * P:(cc + 1) * P].rearrange("p k c -> p c k"))
+                nc.scalar.copy(out=ot_v, in_=stg[j][:, :, cc * P:(cc + 1) * P].rearrange("p k (n i) -> p n k i", i=2))
             elif eng == "g":
-                nc.gpsimd.tensor_scalar(out=ot[:], in0=stg[j][:, :, cc * P:(cc + 1) * P].rearrange("p k c -> p c k"),
+                nc.gpsimd.tensor_scalar(out=ot_v, in0=stg[j][:, :, cc * P:(cc + 1) * P].rearrange("p k (n i) -> p n k i", i=2),
                                         scalar1=1.0, scalar2=0.0, op0=ALU.mult, op1=ALU.add)
             else:
-                nc.vector.tensor_copy(out=ot[:], in_=stg[j][:, :, cc * P:(cc + 1) * P].rearrange("p k c -> p c k"))
+                nc.vector.tensor_copy(out=ot_v, in_=stg[j][:, :, cc * P:(cc + 1) * P].rearrange("p k (n i) -> p n k i", i=2))
             nc.sync.dma_start(out=o1_v[j][:, cc * 1152:(cc + 1) * 1152], in_=ot[:].rearrange("p c k -> p (c k)"))
-
-        w_grp, w_q = {}, {}
-        W_PARTS = [(ch, k, min(k + 2, K9)) for ch in range(4) for k in range(0, K9, 2)]
-
-        def w_interleave(part):
-            ch, k0, k1 = W_PARTS[part]
-            nk = k1 - k0
-            grp = work.tile([P, 2048], BF16, name="wg%d" % part, tag="wg", bufs=4, align_bytes=64)
-            w_grp[part] = grp
-            nc.scalar.copy(out=grp[:, 0:512 * nk].rearrange("p (k c t) -> p c t k", c=P, t=4),
-                           in_=w_raw[ch][:].rearrange("p t (c k) -> p c t k", k=K9)[:, :, :, k0:k1])
-
-        def w_quantize(part):
-            ch, k0, k1 = W_PARTS[part]
-            if k0 == 0:
-                wc = work.tile([P, K9, P], U32, name="w_codes%d" % ch, tag="wc", bufs=5, align_bytes=64)
-                wsc = work.tile([P, K9, P], U8, name="w_scales%d" % ch, tag="ws", bufs=5, align_bytes=64)
-                w_q[ch] = (wc, wsc)
-            codes, scales = w_q[ch]
-            nc.vector.quantize_mx(out=codes[:, k0:k1, :].rearrange("p k c -> p (k c)").bitcast(E4M3),
-                                  scales=scales[:, k0:k1, :].rearrange("p k c -> p (k c)"),
-                                  in_=w_grp[part][:, 0:512 * (k1 - k0)])
 
         m_grp, m_codes = {}, {}
 
         def dz_m_interleave(k, eng):
-            grp = work.tile([P, 2048], BF16, name="mg%d" % k, tag="wg", bufs=4, align_bytes=64)
+            grp = work.tile([P, 2048], BF16, name="mg%d" % k, tag="wg", bufs=WGB, align_bytes=64)
             m_grp[k] = grp
             dst = grp[:].rearrange("p (c i t) -> p c t i", i=4, t=4)
             src = dz[:, k].rearrange("p t (c i) -> p c t i", i=4)
@@ -339,52 +363,48 @@ def tile_psr4convf_v_kernel(tc, x, W, W1, z, grad_out, out_0, out_1):
             gx_seen.append(k)
             for ch in range(4):
                 if len(gx_seen) == 1:
-                    gxp = psum.tile([P, T], F32, name="gx%d" % ch, tag="mm", bufs=4)
+                    tag, nb = ("mm", MMB) if ch < MMB else ("gw", GWB)
+                    gxp = psum.tile([P, T], F32, name="gx%d" % ch, tag=tag, bufs=nb)
                     gx_ps.append(gxp)
                 nc.tensor.matmul_mx(out=gx_ps[ch][:], lhsT=w_q[ch][0][:, k, :].bitcast(E4M3),
                                     lhsT_scale=w_q[ch][1][:, k, :], rhs=codes[:].bitcast(E5M2), rhs_scale=scales[:],
                                     start=(len(gx_seen) == 1), stop=(len(gx_seen) == K9))
 
-        dh_matmul(0)
-        dh_matmul(1)
+        for i in range(DHA):
+            dh_matmul(i)
         todo = []
         next_w = 0
-        for part in range(W_HEAD):
-            w_interleave(part)
-        w_done = 0
+        w_done = W_HEAD_Q
         w_next = W_HEAD
-        for n in range(STEPS + 2):
+        for n in range(STEPS + LQ + 1):
             if n < STEPS:
                 mask(2 * n)
                 mask(2 * n + 1)
                 for i in (2 * n, 2 * n + 1):
                     if i in (8, 17):
                         load_z(i // K9 + 2)
-                for i in (2 * n + 2, 2 * n + 3):
+                for i in (2 * n + DHA, 2 * n + 1 + DHA):
                     if i < 36:
                         dh_matmul(i)
             if 1 <= n <= STEPS:
                 dz_t_copy(n - 1)
-            if w_done < w_next:
+            if w_done < w_next - (W_LAG - 1):
                 w_quantize(w_done)
                 w_done += 1
             if todo:
                 gw_store(*todo.pop(0))
-            if 1 <= n <= STEPS:
-                dz_t_quantize(n - 1)
+            if LQ <= n < STEPS + LQ:
+                dz_t_quantize(n - LQ)
             if n < STEPS:
                 dz_transpose(n)
-            for k, q in M_Q:
-                if q == n:
-                    dz_m_quantize(k)
-            if 2 <= n <= STEPS + 1:
-                for i in (2 * n - 4, 2 * n - 3):
+            if LQ + 1 <= n <= STEPS + LQ:
+                for i in (2 * (n - LQ - 1), 2 * (n - LQ - 1) + 1):
                     gw_copy(i, "v" if i in V_GW else "s")
                     if i % K9 == K9 - 1:
                         todo += [(i // K9, cc) for cc in range(4)]
-            if 1 <= n <= STEPS:
-                gw_matmul(2 * n - 2)
-                gw_matmul(2 * n - 1)
+            if LQ <= n < STEPS + LQ:
+                gw_matmul(2 * (n - LQ))
+                gw_matmul(2 * (n - LQ) + 1)
             if w_next < 20 and n >= W_FROM:
                 w_interleave(w_next)
                 w_next += 1
@@ -393,6 +413,9 @@ def tile_psr4convf_v_kernel(tc, x, W, W1, z, grad_out, out_0, out_1):
             for k, e, q in M_I:
                 if q == n:
                     dz_m_interleave(k, e)
+            for k, q in M_Q:
+                if q == n:
+                    dz_m_quantize(k)
         while w_done < w_next:
             w_quantize(w_done)
             w_done += 1

@@ -19,26 +19,27 @@ RING = [(-1, -1), (-1, 0), (-1, 1), (0, 1), (1, 1), (1, 0), (1, -1), (0, -1)]
 SETS = [(0, 0, 3), (2, 1, 2), (4, 1, 3)]
 STEPS = 18
 S_W1 = ()
-G_W = ()
-V_W = tuple(range(2, 20, 3))
+G_W = tuple(range(4, 20, 2))
+V_W = ()
 V_DY = ()
 W_LAG = 2
-LQ = 1
+LQ = 2
 DHA = 2
-MMB = 4
+MMB = 3
 TRB = 2
-GWB = 2
-TGB = 2
-WGB = 4
+GWB = 3
+TGB = 3
+WGB = 3
 TCB = 3
+VCOLS = 80
 W_HEAD_Q = 0
-W_HEAD = 3
+W_HEAD = 2
 W_FROM = 0
-V_GW = ()
+V_GW = (35,)
 M_I = ()
 M_Q = ()
-TAIL = "s0 v1 k s2 q1 k q0 x1 x0 v3 s4 k q2 x2 q3 x3 k v5 q4 x4 s6 q5 x5 v7 s8 q6 x6 q7 x7 q8 x8".split()
-KLAST = {(j, cc): "v" for j in range(4) for cc in range(4)}
+TAIL = "s0 v1 k s2 q1 k q0 x1 x0 v3 s4 k q2 x2 q3 x3 k v5 q4 x4 s6 q5 x5 v7 q6 x6 b8 q7 x7 q8 x8".split()
+KLAST = {(j, cc): "s" if (j, cc) in ((3, 3),) else "v" for j in range(4) for cc in range(4)}
 TENG = "s"
 
 
@@ -89,16 +90,21 @@ def tile_psr4convf_v_kernel(tc, x, W, W1, z, grad_out, out_0, out_1):
                 nc.sync.dma_start(out=zt[:, 4 * h:4 * h + 4, :], in_=z_v[j][:, 4 * h:4 * h + 4, :])
             z_sb.append(zt)
 
-        def load_g(pr):
-            nc.sync.dma_start(out=g_raw[:, 2 * pr:2 * pr + 2, :], in_=g_v[:, 2 * pr:2 * pr + 2, :])
+        def load_g(b0, b1):
+            nc.sync.dma_start(out=g_raw[:, b0:b1, :], in_=g_v[:, b0:b1, :])
 
-        for pr in range(3):
-            load_g(pr)
-            load_w1(pr)
-        load_g(3)
+        load_g(0, 1)
+        load_g(1, 2)
+        load_w1(0)
+        for b in (2, 4):
+            load_g(b, b + 2)
+            load_w1(b // 2)
+        load_g(6, 8)
         x_raw = work.tile([P, 4, T], BF16, name="x_raw", tag="ot", bufs=3, align_bytes=64)
-        for ct in range(4):
-            nc.sync.dma_start(out=x_raw[:, ct, :].rearrange("p (b n) -> p b n", b=B), in_=x_v[ct])
+
+        def load_x():
+            for ct in range(4):
+                nc.sync.dma_start(out=x_raw[:, ct, :].rearrange("p (b n) -> p b n", b=B), in_=x_v[ct])
 
         base = const.tile([P, K9, 32], BF16, name="base")
         nc.vector.memset(base[:], 0.0)
@@ -113,6 +119,20 @@ def tile_psr4convf_v_kernel(tc, x, W, W1, z, grad_out, out_0, out_1):
             c0, c1 = max(0, dx), min(8, 8 + dx)
             dst = base[:, s, :].rearrange("p (u c) -> p u c", c=8)
             nc.vector.tensor_copy(out=dst[:, u0:u1, c0:c1], in_=stack_v[:, u0 - dy:u1 - dy, c0 - dx:c1 - dx])
+        gs = []
+        for h in range(2):
+            gst = work.tile([P, 3, 4, 512], BF16, name="gs%d" % h, tag=("z", "stg")[h], bufs=2, align_bytes=64)
+            gs.append(gst)
+
+        def g_sort(b0, b1):
+            h, bl = b0 // 4, b0 % 4
+            src = g_raw[:, b0:b1, :].rearrange("p b (m e) -> p (b m) e", e=64)
+            for n, (a, u, rn) in enumerate(SETS):
+                dst = gs[h][:, n, bl:bl + b1 - b0, :].rearrange("p b (m e) -> p (b m) e", e=32)
+                nc.vector.tensor_copy(out=dst, in_=src[:, :, 8 * a:8 * a + 32])
+
+        g_sort(0, 1)
+        g_sort(1, 2)
         rot = const.tile([P, K9, 32], BF16, name="rot")
         for r in range(4):
             rows = slice(32 * r, 32 * r + 32)
@@ -125,18 +145,6 @@ def tile_psr4convf_v_kernel(tc, x, W, W1, z, grad_out, out_0, out_1):
             sh = const.tile([P, K9, 8 * rn], BF16, name="shift%d" % n)
             nc.vector.tensor_copy(out=sh[:], in_=rot[:, :, 8 * u:8 * (u + rn)])
             shift.append(sh)
-
-        gs = []
-        for h in range(2):
-            gst = work.tile([P, 3, 4, 512], BF16, name="gs%d" % h, tag=("z", "stg")[h], bufs=2, align_bytes=64)
-            gs.append(gst)
-
-        def g_sort(pr):
-            h, bl = pr // 2, 2 * (pr % 2)
-            src = g_raw[:, 2 * pr:2 * pr + 2, :].rearrange("p b (m e) -> p (b m) e", e=64)
-            for n, (a, u, rn) in enumerate(SETS):
-                dst = gs[h][:, n, bl:bl + 2, :].rearrange("p b (m e) -> p (b m) e", e=32)
-                nc.vector.tensor_copy(out=dst, in_=src[:, :, 8 * a:8 * a + 32])
 
         dy = big.tile([P, K9, T, 4], BF16, name="dy", tag="dyz", align_bytes=64)
         w1_q = []
@@ -223,28 +231,36 @@ def tile_psr4convf_v_kernel(tc, x, W, W1, z, grad_out, out_0, out_1):
                                   scales=scales[:, k0:k1, :].rearrange("p k c -> p (k c)"),
                                   in_=w_grp[part][:, 0:512 * (k1 - k0)])
 
-        def x_prepare():
-            x_grp = work.tile([P, 2048], BF16, name="x_grp", tag="wg", bufs=WGB, align_bytes=64)
-            x_out = x_grp[:].bitcast(F32).rearrange("p (m n i u) -> p m n i u", m=4, i=2, u=2)
+        x_ps = []
+
+        def x_transpose():
             for h in range(2):
-                tp = psum.tile([P, 2, 2, P], F32, name="xtp%d" % h, tag="tr", bufs=TRB)
+                tp = psum.tile([P, 2, 2, P], F32, name="xtp%d" % h, tag=("tr", "gw")[h], bufs=(TRB, GWB)[h])
+                x_ps.append(tp)
                 for m in range(2):
                     words = x_raw[:, 2 * h + m, :].bitcast(F32)
                     for u in range(2):
                         nc.tensor.transpose(tp[:, m, u, :], words[:, u:256:2], ident_f[:])
-                for m in range(2):
-                    nc.vector.tensor_copy(out=x_out[:, 2 * h + m], in_=tp[:, m].rearrange("p u (i n) -> p n i u", i=2))
+
+        def x_copy():
+            x_grp = work.tile([P, 2048], BF16, name="x_grp", tag="wg", bufs=WGB, align_bytes=64)
+            x_out = x_grp[:].bitcast(F32).rearrange("p (m n i u) -> p m n i u", m=4, i=2, u=2)
+            for m in range(4):
+                nc.vector.tensor_copy(out=x_out[:, m], in_=x_ps[m // 2][:, m % 2].rearrange("p u (i n) -> p n i u", i=2))
             return x_grp
 
-        g_sort(0)
         for b in range(B + 1):
             if b < B:
                 g_transpose(b)
+            if b == B - 1:
+                x_transpose()
             w1_interleave(b)
             if b in (0, 2):
                 load_w1(b // 2 + 3)
             if b in (0, 2, 4):
-                g_sort(b // 2 + 1)
+                g_sort(b + 2, b + 4)
+            if b == 4:
+                load_x()
             if b:
                 w1_quantize(b - 1)
             if b:
@@ -258,7 +274,7 @@ def tile_psr4convf_v_kernel(tc, x, W, W1, z, grad_out, out_0, out_1):
         for k in range(K9):
             dy_quantize(k, 0)
         w1_quantize(8)
-        x_grp = x_prepare()
+        x_grp = x_copy()
         nc.vector.quantize_mx(out=x_codes[:].bitcast(E4M3), scales=x_scales[:], in_=x_grp[:])
         load_w(2)
         for part in range(W_HEAD):
@@ -347,8 +363,11 @@ def tile_psr4convf_v_kernel(tc, x, W, W1, z, grad_out, out_0, out_1):
             src = dz[:, k].rearrange("p t (c i) -> p c t i", i=4)
             if eng == "v":
                 nc.vector.tensor_copy(out=dst, in_=src)
-            else:
+            elif eng == "s":
                 nc.scalar.copy(out=dst, in_=src)
+            else:
+                nc.vector.tensor_copy(out=dst[:, 0:VCOLS], in_=src[:, 0:VCOLS])
+                nc.scalar.copy(out=dst[:, VCOLS:P], in_=src[:, VCOLS:P])
 
         def dz_m_quantize(k):
             codes = work.tile([P, T], U32, name="mc%d" % k, tag="mc", bufs=3, align_bytes=64)

from contextlib import ExitStack

import concourse.mybir as mybir
from concourse.masks import make_identity

F32 = mybir.dt.float32
BF16 = mybir.dt.bfloat16
U32 = mybir.dt.uint32
U8 = mybir.dt.uint8
E4M3 = mybir.dt.float8_e4m3fn_x4
E5M2 = mybir.dt.float8_e5m2_x4
ALU = mybir.AluOpType

B, C, K9, ROT, S = 8, 512, 9, 4, 8
T = B * S * S
P = 128
FLOPS = 3 * 2 * K9 * C * C * T
RING = [(-1, -1), (-1, 0), (-1, 1), (0, 1), (1, 1), (1, 0), (1, -1), (0, -1)]
SETS = [(0, 0, 3), (2, 1, 2), (4, 1, 3)]
STEPS = 18
S_W1 = ()
G_W = tuple(range(4, 20, 2))
V_W = ()
V_DY = ()
W_LAG = 2
LQ = 2
DHA = 2
MMB = 3
TRB = 2
GWB = 3
TGB = 3
WGB = 3
TCB = 3
VCOLS = 80
W_HEAD_Q = 0
W_HEAD = 2
W_FROM = 0
V_GW = (35,)
M_I = ()
M_Q = ()
TAIL = "s0 v1 k s2 q1 k q0 x1 x0 v3 s4 k q2 x2 q3 x3 k v5 q4 x4 s6 q5 x5 v7 q6 x6 b8 q7 x7 q8 x8".split()
KLAST = {(j, cc): "s" if (j, cc) in ((3, 3),) else "v" for j in range(4) for cc in range(4)}
TENG = "s"


def tile_psr4convf_v_kernel(tc, x, W, W1, z, grad_out, out_0, out_1):
    nc = tc.nc
    g_v = grad_out.rearrange("b (q j) r h w -> q b (j r h w)", j=4)
    x_v = x.rearrange("b (c p) h w -> c p b (h w)", p=P)
    w1_v = W1.rearrange("(p j) m -> p j m", j=4)
    w_v = W.rearrange("(p j) c k -> p j (c k)", j=4)
    z_v = z.rearrange("b (p j) k h w -> j p b (k h w)", j=4)
    o1_v = out_1.rearrange("(p j) c k -> j p (c k)", j=4)
    o0_v = out_0.rearrange("b (n p) h w -> n p b (h w)", p=P)

    with ExitStack() as ctx:
        const = ctx.enter_context(tc.tile_pool(name="const", bufs=1))
        big = ctx.enter_context(tc.tile_pool(name="big", bufs=1))
        work = ctx.enter_context(tc.tile_pool(name="work", bufs=2))
        psum = ctx.enter_context(tc.psum_pool(name="psum", bufs=2))

        ident_b = const.tile([P, P], BF16, name="ident_b")
        make_identity(nc, ident_b[:])
        ident_f = const.tile([P, P], F32, name="ident_f")
        make_identity(nc, ident_f[:])

        ctx.enter_context(tc.manual_schedule())

        g_raw = work.tile([P, B, 1024], BF16, name="g_raw", tag="z", bufs=2, align_bytes=64)
        w1_raw = []

        def load_w1(ch):
            k0, nk = max(0, 2 * ch - 1), min(2, 2 * ch + 1)
            raw = work.tile([P, 4, 1152], BF16, name="w1_raw%d" % ch, tag="wraw", bufs=3, align_bytes=64)
            nc.sync.dma_start(out=raw[:, :, 0:nk * 512], in_=w1_v[:, :, 512 * k0:512 * (k0 + nk)])
            w1_raw.append(raw)

        w_raw = []

        def load_w(ch):
            raw = work.tile([P, 4, 1152], BF16, name="w_raw%d" % ch, tag="wraw", bufs=3, align_bytes=64)
            nc.sync.dma_start(out=raw[:], in_=w_v[:, :, ch * 1152:(ch + 1) * 1152])
            w_raw.append(raw)

        z_sb = []

        def load_z(j):
            zt = work.tile([P, B, 576], F32, name="z%d" % j, tag="z", bufs=2, align_bytes=64)
            for h in range(2):
                nc.sync.dma_start(out=zt[:, 4 * h:4 * h + 4, :], in_=z_v[j][:, 4 * h:4 * h + 4, :])
            z_sb.append(zt)

        def load_g(b0, b1):
            nc.sync.dma_start(out=g_raw[:, b0:b1, :], in_=g_v[:, b0:b1, :])

        load_g(0, 1)
        load_g(1, 2)
        load_w1(0)
        for b in (2, 4):
            load_g(b, b + 2)
            load_w1(b // 2)
        load_g(6, 8)
        x_raw = work.tile([P, 4, T], BF16, name="x_raw", tag="ot", bufs=3, align_bytes=64)

        def load_x():
            for ct in range(4):
                nc.sync.dma_start(out=x_raw[:, ct, :].rearrange("p (b n) -> p b n", b=B), in_=x_v[ct])

        base = const.tile([P, K9, 32], BF16, name="base")
        nc.vector.memset(base[:], 0.0)
        stack = const.tile([P, 32], BF16, name="stack")
        for r in range(4):
            rows = slice(32 * r, 32 * r + 32)
            nc.vector.tensor_copy(out=stack[rows, :], in_=ident_b[rows, rows])
        stack_v = stack[:].rearrange("p (u c) -> p u c", c=8)
        for s in range(K9):
            dy, dx = RING[s] if s < 8 else (0, 0)
            u0, u1 = max(0, dy), min(4, 4 + dy)
            c0, c1 = max(0, dx), min(8, 8 + dx)
            dst = base[:, s, :].rearrange("p (u c) -> p u c", c=8)
            nc.vector.tensor_copy(out=dst[:, u0:u1, c0:c1], in_=stack_v[:, u0 - dy:u1 - dy, c0 - dx:c1 - dx])
        gs = []
        for h in range(2):
            gst = work.tile([P, 3, 4, 512], BF16, name="gs%d" % h, tag=("z", "stg")[h], bufs=2, align_bytes=64)
            gs.append(gst)

        def g_sort(b0, b1):
            h, bl = b0 // 4, b0 % 4
            src = g_raw[:, b0:b1, :].rearrange("p b (m e) -> p (b m) e", e=64)
            for n, (a, u, rn) in enumerate(SETS):
                dst = gs[h][:, n, bl:bl + b1 - b0, :].rearrange("p b (m e) -> p (b m) e", e=32)
                nc.vector.tensor_copy(out=dst, in_=src[:, :, 8 * a:8 * a + 32])

        g_sort(0, 1)
        g_sort(1, 2)
        rot = const.tile([P, K9, 32], BF16, name="rot")
        for r in range(4):
            rows = slice(32 * r, 32 * r + 32)
            nc.vector.tensor_copy(out=rot[rows, 0:8 - 2 * r, :], in_=base[rows, 2 * r:8, :])
            if r:
                nc.vector.tensor_copy(out=rot[rows, 8 - 2 * r:8, :], in_=base[rows, 0:2 * r, :])
        nc.vector.tensor_copy(out=rot[:, 8, :], in_=base[:, 8, :])
        shift = []
        for n, (a, u, rn) in enumerate(SETS):
            sh = const.tile([P, K9, 8 * rn], BF16, name="shift%d" % n)
            nc.vector.tensor_copy(out=sh[:], in_=rot[:, :, 8 * u:8 * (u + rn)])
            shift.append(sh)

        dy = big.tile([P, K9, T, 4], BF16, name="dy", tag="dyz", align_bytes=64)
        w1_q = []
        for j in range(4):
            wc = work.tile([P, K9, P], U32, name="w1_codes%d" % j, tag="wc", bufs=5, align_bytes=64)
            wsc = work.tile([P, K9, P], U8, name="w1_scales%d" % j, tag="ws", bufs=5, align_bytes=64)
            w1_q.append((wc, wsc))
        dy_codes = big.tile([P, K9, T], U32, name="dy_codes", align_bytes=64)
        dy_scales = big.tile([P, K9, T], U8, name="dy_scales", align_bytes=64)
        x_codes = big.tile([P, C], U32, name="x_codes", align_bytes=64)
        x_scales = big.tile([P, C], U8, name="x_scales", align_bytes=64)

        g_t = {}

        def g_transpose(b):
            gt = work.tile([P, 3, 4, P], BF16, name="gt%d" % b, tag="tg", bufs=TGB, align_bytes=64)
            g_t[b] = gt
            for n in range(3):
                tp = psum.tile([P, 4, P], BF16, name="gtp%d_%d" % (b, n), tag=("tr", "gw")[(3 * b + n) % 2], bufs=(TRB, GWB)[(3 * b + n) % 2])
                for j in range(4):
                    nc.tensor.transpose(tp[:, j, :], gs[b // 4][:, n, b % 4, j * P:(j + 1) * P], ident_b[:])
                nc.scalar.copy(out=gt[:, n], in_=tp[:])

        def dy_image(b):
            for n, (a, u, rn) in enumerate(SETS):
                nt = 8 * rn
                dp = psum.tile([P, 4, 256], BF16, name="dyp%d_%d" % (b, n), tag="mm", bufs=MMB)
                for j in range(4):
                    nc.tensor.matmul(out=dp[:, j, 0:K9 * nt], lhsT=g_t[b][:, n, j, :],
                                     rhs=shift[n][:].rearrange("p k n -> p (k n)"), start=True, stop=True)
                t0 = 64 * b + 8 * (a + u)
                copy = nc.vector.tensor_copy if (b, n) in V_DY else nc.scalar.copy
                copy(out=dy[:, :, t0:t0 + nt, :],
                               in_=dp[:, :, 0:K9 * nt].rearrange("p j (k n) -> p k n j", k=K9))

        w1_grp = {}

        def w1_interleave(k):
            grp = work.tile([P, 2048], BF16, name="w1g%d" % k, tag="wg", bufs=WGB, align_bytes=64)
            w1_grp[k] = grp
            part = (k + 1) // 2
            k_in = k - max(0, 2 * part - 1)
            raw = w1_raw[part][:, :, 512 * k_in:512 * k_in + 512]
            nc.vector.tensor_copy(
                 out=grp[:].rearrange("p (j n i t) -> p j n t i", j=4, i=2, t=4),
                 in_=raw.rearrange("p t (n i j) -> p j n t i", i=2, j=4))

        def w1_quantize(k):
            for j in range(4):
                codes, scales = w1_q[j]
                nc.vector.quantize_mx(out=codes[:, k, :].bitcast(E4M3), scales=scales[:, k, :],
                                      in_=w1_grp[k][:, 512 * j:512 * j + 512])

        def dy_quantize(k, h):
            ts = slice(256 * h, 256 * h + 256)
            nc.vector.quantize_mx(out=dy_codes[:, k, ts].bitcast(E5M2), scales=dy_scales[:, k, ts],
                                  in_=dy[:, k, ts, :].rearrange("p t j -> p (t j)"))

        w_grp, w_q = {}, {}
        W_PARTS = [(ch, k, min(k + 2, K9)) for ch in range(4) for k in range(0, K9, 2)]

        def w_interleave(part):
            ch, k0, k1 = W_PARTS[part]
            nk = k1 - k0
            grp = work.tile([P, 2048], BF16, name="wg%d" % part, tag="wg", bufs=WGB, align_bytes=64)
            w_grp[part] = grp
            dst = grp[:, 0:512 * nk].rearrange("p (k c t) -> p c t k", c=P, t=4)
            src = w_raw[ch][:].rearrange("p t (c k) -> p c t k", k=K9)[:, :, :, k0:k1]
            if part in G_W:
                nc.gpsimd.tensor_scalar(out=dst, in0=src, scalar1=1.0, scalar2=0.0, op0=ALU.mult, op1=ALU.add)
            elif part in V_W:
                nc.vector.tensor_copy(out=dst, in_=src)
            else:
                nc.scalar.copy(out=dst, in_=src)

        def w_quantize(part):
            ch, k0, k1 = W_PARTS[part]
            if k0 == 0:
                wc = work.tile([P, K9, P], U32, name="w_codes%d" % ch, tag="wc", bufs=5, align_bytes=64)
                wsc = work.tile([P, K9, P], U8, name="w_scales%d" % ch, tag="ws", bufs=5, align_bytes=64)
                w_q[ch] = (wc, wsc)
            codes, scales = w_q[ch]
            nc.vector.quantize_mx(out=codes[:, k0:k1, :].rearrange("p k c -> p (k c)").bitcast(E4M3),
                                  scales=scales[:, k0:k1, :].rearrange("p k c -> p (k c)"),
                                  in_=w_grp[part][:, 0:512 * (k1 - k0)])

        x_ps = []

        def x_transpose():
            for h in range(2):
                tp = psum.tile([P, 2, 2, P], F32, name="xtp%d" % h, tag=("tr", "gw")[h], bufs=(TRB, GWB)[h])
                x_ps.append(tp)
                for m in range(2):
                    words = x_raw[:, 2 * h + m, :].bitcast(F32)
                    for u in range(2):
                        nc.tensor.transpose(tp[:, m, u, :], words[:, u:256:2], ident_f[:])

        def x_copy():
            x_grp = work.tile([P, 2048], BF16, name="x_grp", tag="wg", bufs=WGB, align_bytes=64)
            x_out = x_grp[:].bitcast(F32).rearrange("p (m n i u) -> p m n i u", m=4, i=2, u=2)
            for m in range(4):
                nc.vector.tensor_copy(out=x_out[:, m], in_=x_ps[m // 2][:, m % 2].rearrange("p u (i n) -> p n i u", i=2))
            return x_grp

        for b in range(B + 1):
            if b < B:
                g_transpose(b)
            if b == B - 1:
                x_transpose()
            w1_interleave(b)
            if b in (0, 2):
                load_w1(b // 2 + 3)
            if b in (0, 2, 4):
                g_sort(b + 2, b + 4)
            if b == 4:
                load_x()
            if b:
                w1_quantize(b - 1)
            if b:
                dy_image(b - 1)
            if b == 5:
                load_z(0)
            if b == 7:
                load_w(0)
                load_w(1)
                load_z(1)
        for k in range(K9):
            dy_quantize(k, 0)
        w1_quantize(8)
        x_grp = x_copy()
        nc.vector.quantize_mx(out=x_codes[:].bitcast(E4M3), scales=x_scales[:], in_=x_grp[:])
        load_w(2)
        for part in range(W_HEAD):
            w_interleave(part)
        for part in range(W_HEAD_Q):
            w_quantize(part)
        for k in range(K9):
            dy_quantize(k, 1)

        dz = big.tile([P, K9, 4, T], BF16, name="dz", tag="dyz", align_bytes=64)
        dh_ps, tr_ps, t_grp, t_codes, gw_ps, stg = {}, {}, {}, {}, {}, {}

        def dh_matmul(i):
            j, k = divmod(i, K9)
            ps = psum.tile([P, T], F32, name="dh%d" % i, tag="mm", bufs=MMB)
            dh_ps[i] = ps
            codes, scales = w1_q[j]
            nc.tensor.matmul_mx(out=ps[:], lhsT=codes[:, k, :].bitcast(E4M3), lhsT_scale=scales[:, k, :],
                                rhs=dy_codes[:, k, :].bitcast(E5M2), rhs_scale=dy_scales[:, k, :],
                                start=True, stop=True)

        def mask(i):
            j, k = divmod(i, K9)
            nc.vector.scalar_tensor_tensor(
                out=dz[:, k, j, :].rearrange("p (b n) -> p b n", b=B),
                in0=z_sb[j][:, :, 64 * k:64 * k + 64], scalar=0.0,
                in1=dh_ps[i][:].rearrange("p (b n) -> p b n", b=B),
                op0=ALU.is_gt, op1=ALU.mult)

        def dz_transpose(n):
            tp = psum.tile([P, 2, 2, P], F32, name="trp%d" % n, tag="tr", bufs=TRB)
            tr_ps[n] = tp
            for m in range(2):
                j, k = divmod(2 * n + m, K9)
                words = dz[:, k, j, :].bitcast(F32)
                for u in range(2):
                    nc.tensor.transpose(tp[:, m, u, :], words[:, u:256:2], ident_f[:])

        def dz_t_copy(n):
            grp = work.tile([P, 1024], BF16, name="tg%d" % n, tag="tg", bufs=TGB, align_bytes=64)
            t_grp[n] = grp
            (nc.vector.tensor_copy if TENG == "v" else nc.scalar.copy)(
                out=grp[:].bitcast(F32).rearrange("p (m r u) -> p m r u", m=2, u=2),
                in_=tr_ps[n][:].rearrange("p m u r -> p m r u"))

        def dz_t_quantize(n):
            codes = work.tile([P, 256], U32, name="tc%d" % n, tag="tc", bufs=TCB, align_bytes=64)
            scales = work.tile([P, 256], U8, name="ts%d" % n, tag="ts", bufs=TCB, align_bytes=64)
            t_codes[n] = (codes, scales)
            nc.vector.quantize_mx(out=codes[:].bitcast(E5M2), scales=scales[:], in_=t_grp[n][:])

        def gw_matmul(i):
            codes, scales = t_codes[i // 2]
            cols = slice((i % 2) * P, (i % 2) * P + P)
            ps = psum.tile([P, C], F32, name="gw%d" % i, tag="gw", bufs=GWB)
            gw_ps[i] = ps
            nc.tensor.matmul_mx(out=ps[:], lhsT=codes[:, cols].bitcast(E5M2), lhsT_scale=scales[:, cols],
                                rhs=x_codes[:].bitcast(E4M3), rhs_scale=x_scales[:], start=True, stop=True)

        def gw_copy(i, eng):
            j, k = divmod(i, K9)
            if k == 0:
                stage = work.tile([P, K9, C], F32, name="stg%d" % j, tag="stg", bufs=2, align_bytes=64)
                stg[j] = stage
            (nc.vector.tensor_copy if eng == "v" else nc.scalar.copy)(out=stg[j][:, k, :], in_=gw_ps[i][:])

        def gw_store(j, cc):
            ot = work.tile([P, P, K9], F32, name="ot%d_%d" % (j, cc), tag="ot", bufs=3, align_bytes=64)
            ot_v = ot[:].rearrange("p (i n) k -> p n k i", i=2)
            eng = KLAST[(j, cc)]
            if eng == "s":
                nc.scalar.copy(out=ot_v, in_=stg[j][:, :, cc * P:(cc + 1) * P].rearrange("p k (n i) -> p n k i", i=2))
            elif eng == "g":
                nc.gpsimd.tensor_scalar(out=ot_v, in0=stg[j][:, :, cc * P:(cc + 1) * P].rearrange("p k (n i) -> p n k i", i=2),
                                        scalar1=1.0, scalar2=0.0, op0=ALU.mult, op1=ALU.add)
            else:
                nc.vector.tensor_copy(out=ot_v, in_=stg[j][:, :, cc * P:(cc + 1) * P].rearrange("p k (n i) -> p n k i", i=2))
            nc.sync.dma_start(out=o1_v[j][:, cc * 1152:(cc + 1) * 1152], in_=ot[:].rearrange("p c k -> p (c k)"))

        m_grp, m_codes = {}, {}

        def dz_m_interleave(k, eng):
            grp = work.tile([P, 2048], BF16, name="mg%d" % k, tag="wg", bufs=WGB, align_bytes=64)
            m_grp[k] = grp
            dst = grp[:].rearrange("p (c i t) -> p c t i", i=4, t=4)
            src = dz[:, k].rearrange("p t (c i) -> p c t i", i=4)
            if eng == "v":
                nc.vector.tensor_copy(out=dst, in_=src)
            elif eng == "s":
                nc.scalar.copy(out=dst, in_=src)
            else:
                nc.vector.tensor_copy(out=dst[:, 0:VCOLS], in_=src[:, 0:VCOLS])
                nc.scalar.copy(out=dst[:, VCOLS:P], in_=src[:, VCOLS:P])

        def dz_m_quantize(k):
            codes = work.tile([P, T], U32, name="mc%d" % k, tag="mc", bufs=3, align_bytes=64)
            scales = work.tile([P, T], U8, name="ms%d" % k, tag="ms", bufs=3, align_bytes=64)
            m_codes[k] = (codes, scales)
            nc.vector.quantize_mx(out=codes[:].bitcast(E5M2), scales=scales[:], in_=m_grp[k][:])

        gx_ps, gx_seen = [], []

        def gx_matmul(k):
            codes, scales = m_codes[k]
            gx_seen.append(k)
            for ch in range(4):
                if len(gx_seen) == 1:
                    tag, nb = ("mm", MMB) if ch < MMB else ("gw", GWB)
                    gxp = psum.tile([P, T], F32, name="gx%d" % ch, tag=tag, bufs=nb)
                    gx_ps.append(gxp)
                nc.tensor.matmul_mx(out=gx_ps[ch][:], lhsT=w_q[ch][0][:, k, :].bitcast(E4M3),
                                    lhsT_scale=w_q[ch][1][:, k, :], rhs=codes[:].bitcast(E5M2), rhs_scale=scales[:],
                                    start=(len(gx_seen) == 1), stop=(len(gx_seen) == K9))

        for i in range(DHA):
            dh_matmul(i)
        todo = []
        next_w = 0
        w_done = W_HEAD_Q
        w_next = W_HEAD
        for n in range(STEPS + LQ + 1):
            if n < STEPS:
                mask(2 * n)
                mask(2 * n + 1)
                for i in (2 * n, 2 * n + 1):
                    if i in (8, 17):
                        load_z(i // K9 + 2)
                for i in (2 * n + DHA, 2 * n + 1 + DHA):
                    if i < 36:
                        dh_matmul(i)
            if 1 <= n <= STEPS:
                dz_t_copy(n - 1)
            if w_done < w_next - (W_LAG - 1):
                w_quantize(w_done)
                w_done += 1
            if todo:
                gw_store(*todo.pop(0))
            if LQ <= n < STEPS + LQ:
                dz_t_quantize(n - LQ)
            if n < STEPS:
                dz_transpose(n)
            if LQ + 1 <= n <= STEPS + LQ:
                for i in (2 * (n - LQ - 1), 2 * (n - LQ - 1) + 1):
                    gw_copy(i, "v" if i in V_GW else "s")
                    if i % K9 == K9 - 1:
                        todo += [(i // K9, cc) for cc in range(4)]
            if LQ <= n < STEPS + LQ:
                gw_matmul(2 * (n - LQ))
                gw_matmul(2 * (n - LQ) + 1)
            if w_next < 20 and n >= W_FROM:
                w_interleave(w_next)
                w_next += 1
                if w_next == 6:
                    load_w(3)
            for k, e, q in M_I:
                if q == n:
                    dz_m_interleave(k, e)
            for k, q in M_Q:
                if q == n:
                    dz_m_quantize(k)
        while w_done < w_next:
            w_quantize(w_done)
            w_done += 1
        for item in TAIL:
            if item == "k":
                gw_store(*todo.pop(0))
            elif item[0] == "x":
                gx_matmul(int(item[1]))
            elif item[0] == "q":
                dz_m_quantize(int(item[1]))
            else:
                dz_m_interleave(int(item[1]), item[0])
        gx_out = work.tile([P, 4, T], F32, name="gx_out", tag="stg", bufs=2, align_bytes=64)
        for ch in range(4):
            if ch % 2:
                nc.vector.tensor_copy(out=gx_out[:, ch, :], in_=gx_ps[ch][:])
            else:
                nc.scalar.copy(out=gx_out[:, ch, :], in_=gx_ps[ch][:])
            nc.sync.dma_start(out=o0_v[ch], in_=gx_out[:, ch, :].rearrange("p (b n) -> p b n", b=B))
